import numpy as np
import ml_dtypes


def mxq(x, axis, fmt="e4m3"):
    dtype, down = {"e4m3": (ml_dtypes.float8_e4m3fn, 7), "e5m2": (ml_dtypes.float8_e5m2, 14)}[fmt]
    v = np.moveaxis(np.asarray(x, np.float32).astype(ml_dtypes.bfloat16).astype(np.float64), axis, -1)
    blocks = v.reshape(v.shape[:-1] + (-1, 32))
    amax = np.abs(blocks).max(-1, keepdims=True)
    byte = np.maximum(np.where(amax > 0, np.frexp(amax)[1] - 1 + 127, 0) - down, 1)
    scale = np.exp2(byte - 127.0)
    codes = (blocks / scale).astype(np.float32).astype(dtype).astype(np.float64)
    return np.moveaxis((codes * scale).reshape(v.shape), -1, axis)


WIDE = False


def mx_kscale(k):
    if not WIDE:
        return np.ones(k)
    levels = np.array([10, -10, 5, -5, 0])
    if k % 512:
        return np.exp2(np.random.permutation(np.resize(levels, k // 32))).repeat(32)
    a = np.empty((k // 512, 16))
    for p in range(k // 512):
        a[p, :8] = np.random.permutation(np.resize(levels, 8))
        for g in range(8):
            far = levels[np.abs(levels - a[p, g]) >= 10]
            a[p, g + 8] = far[np.random.randint(len(far))]
    return np.exp2(a.ravel()).repeat(32)


BF16 = ml_dtypes.bfloat16


def bf(x):
    return np.asarray(x, np.float32).astype(BF16)


def f64(x):
    return np.asarray(x).astype(np.float64)


B, T, DM, DH, L = 4, 512, 1024, 1024, 512


def setup_inputs():
    s, u = mx_kscale(DM), mx_kscale(DM)
    return {"k": bf(np.random.standard_normal((B, T, DM)) * s),
            "v": bf(np.random.standard_normal((B, T, DM)) * u),
            "Wk": bf(np.random.standard_normal((DH, DM)) / np.sqrt(DM) / s),
            "Wv": bf(np.random.standard_normal((DH, DM)) * 3.0 / np.sqrt(DM) / u)}


def reference(k, v, Wk, Wv):
    K = mxq(f64(k), 2, "e4m3") @ mxq(f64(Wk), 1, "e4m3").T
    V = mxq(f64(v), 2, "e4m3") @ mxq(f64(Wv), 1, "e4m3").T
    max_key = K.max(axis=0, keepdims=True)
    exp_key = np.exp(K - max_key)
    return exp_key * V, exp_key

@@ -1,0 +1,248 @@
+from contextlib import ExitStack
+
+import concourse.mybir as mybir
+from concourse.masks import make_identity
+
+F32 = mybir.dt.float32
+BF16 = mybir.dt.bfloat16
+U32 = mybir.dt.uint32
+U8 = mybir.dt.uint8
+FP8X4 = mybir.dt.float8_e4m3fn_x4
+ALU = mybir.AluOpType
+ACT = mybir.ActivationFunctionType
+
+P = 128
+B, T, DM, DH = 4, 512, 1024, 1024
+PACK = 4
+K_PASS = P * PACK
+PASSES = DM // K_PASS
+PAIRS = DM // 2
+SLOTS = PAIRS // P
+BLOCKS = 4
+CHUNK = BLOCKS * P
+N = 512
+HALVES = DH // N
+TOKEN_TILES = T // P
+GROUPS = TOKEN_TILES * HALVES
+K_SIDE = 0
+V_SIDE = 1
+
+BANKS = {"k0_v1": 1, "k2_v3": 1, "k1": 1, "k3": 1, "turn_v0": 2, "turn_v2": 2}
+K_BANK = {0: "k0_v1", 1: "k1", 2: "k2_v3", 3: "k3"}
+V_BANK = {0: "turn_v0", 1: "k0_v1", 2: "turn_v2", 3: "k2_v3"}
+TURN_BANK = ("turn_v0", "turn_v2")
+
+FLOPS = 2 * 2 * B * T * DM * DH
+
+
+def chunks_first_used_by(side, group):
+    found = []
+    if 0 <= group < GROUPS:
+        token_tile, half = divmod(group, HALVES)
+        if token_tile == 0:
+            found.append((side, "weights", half))
+        if half == 0:
+            found.append((side, "tokens", token_tile))
+    return found
+
+
+def tile_aftfull_pa_kernel(tc, k, v, Wk, Wv, out_0, out_1):
+    nc = tc.nc
+    tokens = (k, v)
+    weights = (Wk, Wv)
+
+    first_chunks = (
+        chunks_first_used_by(K_SIDE, 0) + chunks_first_used_by(K_SIDE, 1) + chunks_first_used_by(V_SIDE, 0)
+    )
+    chunks_of_period = [
+        chunks_first_used_by(K_SIDE, period + 2) + chunks_first_used_by(V_SIDE, period + 1)
+        for period in range(GROUPS + 1)
+    ]
+
+    with ExitStack() as stack:
+        const_pool = stack.enter_context(tc.tile_pool(name="const", bufs=1))
+        raw_pool = stack.enter_context(tc.tile_pool(name="raw", bufs=20))
+        grouped_pool = stack.enter_context(tc.tile_pool(name="grouped", bufs=2))
+        mx_pool = stack.enter_context(tc.tile_pool(name="mx", bufs=1))
+        work_pool = stack.enter_context(tc.tile_pool(name="work", bufs=2))
+        e_pool = stack.enter_context(tc.tile_pool(name="e", bufs=3))
+        ev_pool = stack.enter_context(tc.tile_pool(name="ev", bufs=1))
+        psum = stack.enter_context(tc.psum_pool(name="psum", bufs=1))
+
+        identity = const_pool.tile([P, P], F32, name="identity")
+        make_identity(nc, identity[:])
+
+        stack.enter_context(tc.manual_schedule())
+
+        warm = const_pool.tile([P, 1], F32, name="warm")
+        nc.vector.memset(warm[:], 0.0)
+        nc.scalar.activation(out=warm[:], in_=warm[:], func=ACT.Exp)
+
+        raw = {}
+        grouped = {}
+        codes = {}
+        scales = {}
+        e_tiles = {}
+        ev_tiles = {}
+
+        def bank(name):
+            return psum.tile([P, N], F32, name=name, tag=name, bufs=BANKS[name])
+
+        def load(chunk):
+            side, kind, index = chunk
+            for block in range(BLOCKS):
+                if kind == "weights":
+                    first = index * CHUNK + block * P
+                    rows = weights[side][first : first + P, :]
+                else:
+                    rows = tokens[side][block, index * P : (index + 1) * P, :]
+                raw[(chunk, block)] = raw_pool.tile([P, DM], BF16, name="raw", tag="raw")
+                nc.sync.dma_start(out=raw[(chunk, block)][:], in_=rows)
+
+        def turn(chunk, block):
+            if block == 0:
+                grouped[chunk] = grouped_pool.tile(
+                    [P, PASSES * CHUNK * PACK], BF16, name="grouped", tag="grouped", align_bytes=64
+                )
+            words = raw[(chunk, block)][:].bitcast(F32)
+            turned = bank(TURN_BANK[block % 2])
+            for q in range(SLOTS):
+                g, u = divmod(q, 2)
+                picked = words[:, 2 * P * g + u : 2 * P * (g + 1) : 2]
+                nc.tensor.transpose(turned[:, q * P : (q + 1) * P], picked, identity[:])
+            pairs = grouped[chunk][:].bitcast(F32).rearrange("p (g r u) -> p g r u", g=PASSES, u=2)
+            nc.scalar.copy(
+                out=pairs[:, :, block * P : (block + 1) * P, :],
+                in_=turned[:].rearrange("p (g u r) -> p g r u", g=PASSES, u=2),
+            )
+
+        def quantise(chunk):
+            name = "%d_%s_%d" % chunk
+            codes[chunk] = mx_pool.tile([P, PASSES, CHUNK], U32, name="codes_" + name, align_bytes=64)
+            scales[chunk] = mx_pool.tile([P, PASSES, CHUNK], U8, name="scales_" + name, align_bytes=64)
+            nc.vector.quantize_mx(
+                out=codes[chunk][:].rearrange("p g r -> p (g r)").bitcast(FP8X4),
+                scales=scales[chunk][:].rearrange("p g r -> p (g r)"),
+                in_=grouped[chunk][:],
+            )
+
+        def product(side, group, b):
+            token_tile, half = divmod(group, HALVES)
+            x = (side, "tokens", token_tile)
+            w = (side, "weights", half)
+            rows = slice(b * P, (b + 1) * P)
+            acc = bank(K_BANK[b] if side == K_SIDE else V_BANK[b])
+            for g in range(PASSES):
+                nc.tensor.matmul_mx(
+                    out=acc[:],
+                    lhsT=codes[x][:, g, rows].bitcast(FP8X4),
+                    lhsT_scale=scales[x][:, g, rows],
+                    rhs=codes[w][:, g, :].bitcast(FP8X4),
+                    rhs_scale=scales[w][:, g, :],
+                    start=(g == 0),
+                    stop=(g == PASSES - 1),
+                )
+            return acc
+
+        def k_products(group):
+            big_k = {}
+            for b in (0, 2, 1, 3):
+                big_k[b] = product(K_SIDE, group, b)
+            k_copy = work_pool.tile([P, 2, N], F32, name="k_copy")
+            for b in (0, 2):
+                nc.scalar.copy(out=k_copy[:, b // 2, :], in_=big_k[b][:])
+            return big_k, k_copy
+
+        def pair_in(out, group, parity):
+            token_tile, half = divmod(group, HALVES)
+            part = out[parity:B:2, token_tile * P : (token_tile + 1) * P, half * N : (half + 1) * N]
+            return part.rearrange("b p c -> p b c")
+
+        def exp_and_store(group, parity):
+            e = e_tiles[(group, parity)]
+            flat = e[:].rearrange("p b c -> p (b c)")
+            nc.scalar.activation(out=flat, in_=flat, func=ACT.Exp)
+            nc.sync.dma_start(out=pair_in(out_1, group, parity), in_=e[:])
+
+        def multiply(group, b, big_v):
+            parity = b % 2
+            if b == parity:
+                ev_tiles[(group, parity)] = ev_pool.tile([P, 2, N], F32, name="ev_%d_%d" % (group, parity))
+            nc.vector.tensor_tensor(
+                out=ev_tiles[(group, parity)][:, b // 2, :],
+                in0=big_v[:],
+                in1=e_tiles[(group, parity)][:, b // 2, :],
+                op=ALU.mult,
+            )
+            if b == parity + 2:
+                nc.sync.dma_start(out=pair_in(out_0, group, parity), in_=ev_tiles[(group, parity)][:])
+
+        for chunk in first_chunks:
+            load(chunk)
+        for chunks in chunks_of_period:
+            for chunk in chunks:
+                load(chunk)
+
+        for i, chunk in enumerate(first_chunks):
+            for block in range(BLOCKS):
+                turn(chunk, block)
+            if i > 0:
+                quantise(first_chunks[i - 1])
+        quantise(first_chunks[-1])
+        big_k, k_copy = k_products(0)
+
+        for period in range(GROUPS + 1):
+            group = period
+            v_group = period - 1
+            has_k = group < GROUPS
+            has_v = v_group >= 0
+            blocks = [(chunk, block) for chunk in chunks_of_period[period] for block in range(BLOCKS)]
+            middle = len(blocks) // 2
+            big_v = {}
+
+            if has_v:
+                for b in (1, 3):
+                    big_v[b] = product(V_SIDE, v_group, b)
+
+            if has_k:
+                max_01 = work_pool.tile([P, N], F32, name="max_01")
+                max_23 = work_pool.tile([P, N], F32, name="max_23")
+                max_all = work_pool.tile([P, N], F32, name="max_all")
+                nc.vector.tensor_tensor(out=max_01[:], in0=big_k[1][:], in1=k_copy[:, 0, :], op=ALU.max)
+                nc.vector.tensor_tensor(out=max_23[:], in0=big_k[3][:], in1=k_copy[:, 1, :], op=ALU.max)
+            if has_v:
+                multiply(v_group, 1, big_v[1])
+            if has_k:
+                nc.vector.tensor_tensor(out=max_all[:], in0=max_01[:], in1=max_23[:], op=ALU.max)
+            if has_v:
+                multiply(v_group, 3, big_v[3])
+            if has_k:
+                for parity in (0, 1):
+                    e_tiles[(group, parity)] = e_pool.tile([P, 2, N], F32, name="e_%d" % parity)
+                for b in (1, 3):
+                    nc.vector.tensor_tensor(
+                        out=e_tiles[(group, 1)][:, b // 2, :], in0=big_k[b][:], in1=max_all[:], op=ALU.subtract
+                    )
+                for b in (0, 2):
+                    nc.gpsimd.tensor_tensor(
+                        out=e_tiles[(group, 0)][:, b // 2, :], in0=k_copy[:, b // 2, :], in1=max_all[:], op=ALU.subtract
+                    )
+
+            for chunk, block in blocks[:middle]:
+                turn(chunk, block)
+            if has_v:
+                exp_and_store(v_group, 0)
+                for b in (0, 2):
+                    big_v[b] = product(V_SIDE, v_group, b)
+                for b in (0, 2):
+                    multiply(v_group, b, big_v[b])
+            for chunk, block in blocks[middle:]:
+                turn(chunk, block)
+            for chunk in chunks_of_period[period]:
+                quantise(chunk)
+            if group + 1 < GROUPS:
+                big_k_next, k_copy_next = k_products(group + 1)
+            if has_k:
+                exp_and_store(group, 1)
+            if group + 1 < GROUPS:
+                big_k, k_copy = big_k_next, k_copy_next

@@ -22,6 +22,7 @@ BLOCKS = 4
 CHUNK = BLOCKS * P
 N = 512
 HALVES = DH // N
+SORTED_BLOCKS = (1, 3)
 TOKEN_TILES = T // P
 GROUPS = TOKEN_TILES * HALVES
 K_SIDE = 0
@@ -62,6 +63,7 @@ def tile_aftfull_pa_kernel(tc, k, v, Wk, Wv, out_0, out_1):
     with ExitStack() as stack:
         const_pool = stack.enter_context(tc.tile_pool(name="const", bufs=1))
         raw_pool = stack.enter_context(tc.tile_pool(name="raw", bufs=20))
+        sorted_pool = stack.enter_context(tc.tile_pool(name="sorted", bufs=4))
         grouped_pool = stack.enter_context(tc.tile_pool(name="grouped", bufs=2))
         mx_pool = stack.enter_context(tc.tile_pool(name="mx", bufs=1))
         work_pool = stack.enter_context(tc.tile_pool(name="work", bufs=2))
@@ -79,6 +81,7 @@ def tile_aftfull_pa_kernel(tc, k, v, Wk, Wv, out_0, out_1):
         nc.scalar.activation(out=warm[:], in_=warm[:], func=ACT.Exp)
 
         raw = {}
+        sorted_words = {}
         grouped = {}
         codes = {}
         scales = {}
@@ -99,6 +102,13 @@ def tile_aftfull_pa_kernel(tc, k, v, Wk, Wv, out_0, out_1):
                 raw[(chunk, block)] = raw_pool.tile([P, DM], BF16, name="raw", tag="raw")
                 nc.sync.dma_start(out=raw[(chunk, block)][:], in_=rows)
 
+        def sort(chunk, block):
+            sorted_words[(chunk, block)] = sorted_pool.tile([P, PASSES, 2, P], F32, name="sorted", tag="sorted")
+            nc.vector.tensor_copy(
+                out=sorted_words[(chunk, block)][:],
+                in_=raw[(chunk, block)][:].bitcast(F32).rearrange("p (g m u) -> p g u m", g=PASSES, u=2),
+            )
+
         def turn(chunk, block):
             if block == 0:
                 grouped[chunk] = grouped_pool.tile(
@@ -108,7 +118,10 @@ def tile_aftfull_pa_kernel(tc, k, v, Wk, Wv, out_0, out_1):
             turned = bank(TURN_BANK[block % 2])
             for q in range(SLOTS):
                 g, u = divmod(q, 2)
-                picked = words[:, 2 * P * g + u : 2 * P * (g + 1) : 2]
+                if (chunk, block) in sorted_words:
+                    picked = sorted_words[(chunk, block)][:, g, u, :]
+                else:
+                    picked = words[:, 2 * P * g + u : 2 * P * (g + 1) : 2]
                 nc.tensor.transpose(turned[:, q * P : (q + 1) * P], picked, identity[:])
             pairs = grouped[chunk][:].bitcast(F32).rearrange("p (g r u) -> p g r u", g=PASSES, u=2)
             nc.scalar.copy(
@@ -238,6 +251,10 @@ def tile_aftfull_pa_kernel(tc, k, v, Wk, Wv, out_0, out_1):
                     multiply(v_group, b, big_v[b])
             for chunk, block in blocks[middle:]:
                 turn(chunk, block)
+            if group < GROUPS:
+                for chunk in chunks_of_period[period + 1]:
+                    for block in SORTED_BLOCKS:
+                        sort(chunk, block)
             for chunk in chunks_of_period[period]:
                 quantise(chunk)
             if group + 1 < GROUPS:

@@ -22,7 +22,7 @@ BLOCKS = 4
 CHUNK = BLOCKS * P
 N = 512
 HALVES = DH // N
-SORTED_BLOCKS = (1, 3)
+SORTED_BLOCKS = (1,)
 TOKEN_TILES = T // P
 GROUPS = TOKEN_TILES * HALVES
 K_SIDE = 0
@@ -59,6 +59,8 @@ def tile_aftfull_pa_kernel(tc, k, v, Wk, Wv, out_0, out_1):
         chunks_first_used_by(K_SIDE, period + 2) + chunks_first_used_by(V_SIDE, period + 1)
         for period in range(GROUPS + 1)
     ]
+    chunks_of_period[GROUPS - 2] += chunks_of_period[GROUPS - 3]
+    chunks_of_period[GROUPS - 3] = []
 
     with ExitStack() as stack:
         const_pool = stack.enter_context(tc.tile_pool(name="const", bufs=1))
@@ -187,7 +189,10 @@ def tile_aftfull_pa_kernel(tc, k, v, Wk, Wv, out_0, out_1):
                 in1=e_tiles[(group, parity)][:, b // 2, :],
                 op=ALU.mult,
             )
-            if b == parity + 2:
+            if group // HALVES == TOKEN_TILES - 1:
+                part = pair_in(out_0, group, parity)[:, b // 2, :]
+                nc.sync.dma_start(out=part, in_=ev_tiles[(group, parity)][:, b // 2, :])
+            elif b == parity + 2:
                 nc.sync.dma_start(out=pair_in(out_0, group, parity), in_=ev_tiles[(group, parity)][:])
 
         for chunk in first_chunks:
@@ -202,6 +207,9 @@ def tile_aftfull_pa_kernel(tc, k, v, Wk, Wv, out_0, out_1):
             if i > 0:
                 quantise(first_chunks[i - 1])
         quantise(first_chunks[-1])
+        for chunk in chunks_of_period[0]:
+            for block in range(BLOCKS):
+                sort(chunk, block)
         big_k, k_copy = k_products(0)
 
         for period in range(GROUPS + 1):

@@ -104,9 +104,9 @@ def tile_aftfull_pa_kernel(tc, k, v, Wk, Wv, out_0, out_1):
                 raw[(chunk, block)] = raw_pool.tile([P, DM], BF16, name="raw", tag="raw")
                 nc.sync.dma_start(out=raw[(chunk, block)][:], in_=rows)
 
-        def sort(chunk, block):
+        def sort(chunk, block, copy):
             sorted_words[(chunk, block)] = sorted_pool.tile([P, PASSES, 2, P], F32, name="sorted", tag="sorted")
-            nc.vector.tensor_copy(
+            copy(
                 out=sorted_words[(chunk, block)][:],
                 in_=raw[(chunk, block)][:].bitcast(F32).rearrange("p (g m u) -> p g u m", g=PASSES, u=2),
             )
@@ -209,7 +209,7 @@ def tile_aftfull_pa_kernel(tc, k, v, Wk, Wv, out_0, out_1):
         quantise(first_chunks[-1])
         for chunk in chunks_of_period[0]:
             for block in range(BLOCKS):
-                sort(chunk, block)
+                sort(chunk, block, nc.vector.tensor_copy)
         big_k, k_copy = k_products(0)
 
         for period in range(GROUPS + 1):
@@ -253,16 +253,16 @@ def tile_aftfull_pa_kernel(tc, k, v, Wk, Wv, out_0, out_1):
                 turn(chunk, block)
             if has_v:
                 exp_and_store(v_group, 0)
+                if period + 1 < GROUPS - 2:
+                    for chunk in chunks_of_period[period + 1]:
+                        for block in SORTED_BLOCKS:
+                            sort(chunk, block, nc.scalar.copy)
                 for b in (0, 2):
                     big_v[b] = product(V_SIDE, v_group, b)
                 for b in (0, 2):
                     multiply(v_group, b, big_v[b])
             for chunk, block in blocks[middle:]:
                 turn(chunk, block)
-            if group < GROUPS:
-                for chunk in chunks_of_period[period + 1]:
-                    for block in SORTED_BLOCKS:
-                        sort(chunk, block)
             for chunk in chunks_of_period[period]:
                 quantise(chunk)
             if group + 1 < GROUPS:

@@ -22,7 +22,7 @@ BLOCKS = 4
 CHUNK = BLOCKS * P
 N = 512
 HALVES = DH // N
-SORTED_BLOCKS = (1,)
+SORTED_BLOCKS = (0,)
 TOKEN_TILES = T // P
 GROUPS = TOKEN_TILES * HALVES
 K_SIDE = 0
@@ -87,6 +87,10 @@ def tile_aftfull_pa_kernel(tc, k, v, Wk, Wv, out_0, out_1):
         grouped = {}
         codes = {}
         scales = {}
+        big_k = {}
+        k_copies = {}
+        pair_max = {}
+        max_all = {}
         e_tiles = {}
         ev_tiles = {}
 
@@ -159,14 +163,50 @@ def tile_aftfull_pa_kernel(tc, k, v, Wk, Wv, out_0, out_1):
                 )
             return acc
 
-        def k_products(group):
-            big_k = {}
-            for b in (0, 2, 1, 3):
-                big_k[b] = product(K_SIDE, group, b)
-            k_copy = work_pool.tile([P, 2, N], F32, name="k_copy")
+        def k_products(group, items):
+            if group not in k_copies:
+                k_copies[group] = work_pool.tile([P, 2, N], F32, name="k_copy")
+            for b in items:
+                big_k[(group, b)] = product(K_SIDE, group, b)
+            for b in items:
+                if b % 2 == 0:
+                    nc.scalar.copy(out=k_copies[group][:, b // 2, :], in_=big_k[(group, b)][:])
+
+        def pair_maxima(group):
+            pair_max[group] = []
+            for first, name in ((0, "max_01"), (2, "max_23")):
+                pair = work_pool.tile([P, N], F32, name=name)
+                nc.vector.tensor_tensor(
+                    out=pair[:],
+                    in0=big_k[(group, first + 1)][:],
+                    in1=k_copies[group][:, first // 2, :],
+                    op=ALU.max,
+                )
+                pair_max[group].append(pair)
+
+        def maximum(group):
+            max_all[group] = work_pool.tile([P, N], F32, name="max_all")
+            nc.vector.tensor_tensor(
+                out=max_all[group][:], in0=pair_max[group][0][:], in1=pair_max[group][1][:], op=ALU.max
+            )
+
+        def differences(group):
+            for parity in (0, 1):
+                e_tiles[(group, parity)] = e_pool.tile([P, 2, N], F32, name="e_%d" % parity)
+            for b in (1, 3):
+                nc.vector.tensor_tensor(
+                    out=e_tiles[(group, 1)][:, b // 2, :],
+                    in0=big_k[(group, b)][:],
+                    in1=max_all[group][:],
+                    op=ALU.subtract,
+                )
             for b in (0, 2):
-                nc.scalar.copy(out=k_copy[:, b // 2, :], in_=big_k[b][:])
-            return big_k, k_copy
+                nc.gpsimd.tensor_tensor(
+                    out=e_tiles[(group, 0)][:, b // 2, :],
+                    in0=k_copies[group][:, b // 2, :],
+                    in1=max_all[group][:],
+                    op=ALU.subtract,
+                )
 
         def pair_in(out, group, parity):
             token_tile, half = divmod(group, HALVES)
@@ -206,68 +246,63 @@ def tile_aftfull_pa_kernel(tc, k, v, Wk, Wv, out_0, out_1):
                 turn(chunk, block)
             if i > 0:
                 quantise(first_chunks[i - 1])
-        quantise(first_chunks[-1])
-        for chunk in chunks_of_period[0]:
-            for block in range(BLOCKS):
-                sort(chunk, block, nc.vector.tensor_copy)
-        big_k, k_copy = k_products(0)
 
-        for period in range(GROUPS + 1):
+        early, late = chunks_of_period[0]
+        for block in range(BLOCKS):
+            if block == BLOCKS // 2:
+                quantise(first_chunks[-1])
+            sort(early, block, nc.vector.tensor_copy)
+        k_products(0, (0, 2, 1, 3))
+        pair_maxima(0)
+        for block in range(BLOCKS):
+            sort(late, block, nc.vector.tensor_copy)
+        maximum(0)
+        differences(0)
+        for block in range(BLOCKS):
+            turn(early, block)
+        k_products(1, (0, 2))
+        for block in range(BLOCKS):
+            turn(late, block)
+        k_products(1, (1, 3))
+        exp_and_store(0, 1)
+
+        for period in range(1, GROUPS + 1):
             group = period
             v_group = period - 1
             has_k = group < GROUPS
-            has_v = v_group >= 0
             blocks = [(chunk, block) for chunk in chunks_of_period[period] for block in range(BLOCKS)]
             middle = len(blocks) // 2
             big_v = {}
 
-            if has_v:
-                for b in (1, 3):
-                    big_v[b] = product(V_SIDE, v_group, b)
-
+            big_v[1] = product(V_SIDE, v_group, 1)
             if has_k:
-                max_01 = work_pool.tile([P, N], F32, name="max_01")
-                max_23 = work_pool.tile([P, N], F32, name="max_23")
-                max_all = work_pool.tile([P, N], F32, name="max_all")
-                nc.vector.tensor_tensor(out=max_01[:], in0=big_k[1][:], in1=k_copy[:, 0, :], op=ALU.max)
-                nc.vector.tensor_tensor(out=max_23[:], in0=big_k[3][:], in1=k_copy[:, 1, :], op=ALU.max)
-            if has_v:
-                multiply(v_group, 1, big_v[1])
-            if has_k:
-                nc.vector.tensor_tensor(out=max_all[:], in0=max_01[:], in1=max_23[:], op=ALU.max)
-            if has_v:
-                multiply(v_group, 3, big_v[3])
-            if has_k:
-                for parity in (0, 1):
-                    e_tiles[(group, parity)] = e_pool.tile([P, 2, N], F32, name="e_%d" % parity)
-                for b in (1, 3):
-                    nc.vector.tensor_tensor(
-                        out=e_tiles[(group, 1)][:, b // 2, :], in0=big_k[b][:], in1=max_all[:], op=ALU.subtract
-                    )
-                for b in (0, 2):
-                    nc.gpsimd.tensor_tensor(
-                        out=e_tiles[(group, 0)][:, b // 2, :], in0=k_copy[:, b // 2, :], in1=max_all[:], op=ALU.subtract
-                    )
-
+                pair_maxima(group)
+            if period == 1:
+                for chunk in chunks_of_period[0]:
+                    quantise(chunk)
+            multiply(v_group, 1, big_v[1])
             for chunk, block in blocks[:middle]:
                 turn(chunk, block)
-            if has_v:
-                exp_and_store(v_group, 0)
-                if period + 1 < GROUPS - 2:
-                    for chunk in chunks_of_period[period + 1]:
-                        for block in SORTED_BLOCKS:
-                            sort(chunk, block, nc.scalar.copy)
-                for b in (0, 2):
-                    big_v[b] = product(V_SIDE, v_group, b)
-                for b in (0, 2):
-                    multiply(v_group, b, big_v[b])
+            big_v[3] = product(V_SIDE, v_group, 3)
+            if has_k:
+                maximum(group)
+            multiply(v_group, 3, big_v[3])
+            if period < GROUPS:
+                for chunk in chunks_of_period[period + 1]:
+                    for block in SORTED_BLOCKS:
+                        sort(chunk, block, nc.scalar.copy)
+            exp_and_store(v_group, 0)
+            if has_k:
+                differences(group)
             for chunk, block in blocks[middle:]:
                 turn(chunk, block)
+            for b in (0, 2):
+                big_v[b] = product(V_SIDE, v_group, b)
+            for b in (0, 2):
+                multiply(v_group, b, big_v[b])
             for chunk in chunks_of_period[period]:
                 quantise(chunk)
             if group + 1 < GROUPS:
-                big_k_next, k_copy_next = k_products(group + 1)
+                k_products(group + 1, (0, 2, 1, 3))
             if has_k:
                 exp_and_store(group, 1)
-            if group + 1 < GROUPS:
-                big_k, k_copy = big_k_next, k_copy_next

@@ -22,7 +22,8 @@ BLOCKS = 4
 CHUNK = BLOCKS * P
 N = 512
 HALVES = DH // N
-SORTED_BLOCKS = (0,)
+SORTED_BY_SCALAR = (0,)
+SORTED_BY_GPSIMD = {2: (2, 3)}
 TOKEN_TILES = T // P
 GROUPS = TOKEN_TILES * HALVES
 K_SIDE = 0
@@ -88,6 +89,7 @@ def tile_aftfull_pa_kernel(tc, k, v, Wk, Wv, out_0, out_1):
         codes = {}
         scales = {}
         big_k = {}
+        even_copies = {}
         k_copies = {}
         pair_max = {}
         max_all = {}
@@ -163,24 +165,25 @@ def tile_aftfull_pa_kernel(tc, k, v, Wk, Wv, out_0, out_1):
                 )
             return acc
 
-        def k_products(group, items):
-            if group not in k_copies:
-                k_copies[group] = work_pool.tile([P, 2, N], F32, name="k_copy")
+        def k_products(group, items, copied):
             for b in items:
                 big_k[(group, b)] = product(K_SIDE, group, b)
-            for b in items:
+            for b in copied:
                 if b % 2 == 0:
-                    nc.scalar.copy(out=k_copies[group][:, b // 2, :], in_=big_k[(group, b)][:])
+                    if group not in even_copies:
+                        even_copies[group] = work_pool.tile([P, 2, N], F32, name="k_copy")
+                    k_copies[(group, b)] = even_copies[group][:, b // 2, :]
+                else:
+                    odd_copy = work_pool.tile([P, N], F32, name="k_copy_1", bufs=1)
+                    k_copies[(group, b)] = odd_copy[:]
+                nc.scalar.copy(out=k_copies[(group, b)], in_=big_k[(group, b)][:])
 
         def pair_maxima(group):
             pair_max[group] = []
             for first, name in ((0, "max_01"), (2, "max_23")):
                 pair = work_pool.tile([P, N], F32, name=name)
                 nc.vector.tensor_tensor(
-                    out=pair[:],
-                    in0=big_k[(group, first + 1)][:],
-                    in1=k_copies[group][:, first // 2, :],
-                    op=ALU.max,
+                    out=pair[:], in0=big_k[(group, first + 1)][:], in1=k_copies[(group, first)], op=ALU.max
                 )
                 pair_max[group].append(pair)
 
@@ -189,24 +192,16 @@ def tile_aftfull_pa_kernel(tc, k, v, Wk, Wv, out_0, out_1):
             nc.vector.tensor_tensor(
                 out=max_all[group][:], in0=pair_max[group][0][:], in1=pair_max[group][1][:], op=ALU.max
             )
-
-        def differences(group):
             for parity in (0, 1):
                 e_tiles[(group, parity)] = e_pool.tile([P, 2, N], F32, name="e_%d" % parity)
-            for b in (1, 3):
-                nc.vector.tensor_tensor(
-                    out=e_tiles[(group, 1)][:, b // 2, :],
-                    in0=big_k[(group, b)][:],
-                    in1=max_all[group][:],
-                    op=ALU.subtract,
-                )
-            for b in (0, 2):
-                nc.gpsimd.tensor_tensor(
-                    out=e_tiles[(group, 0)][:, b // 2, :],
-                    in0=k_copies[group][:, b // 2, :],
-                    in1=max_all[group][:],
-                    op=ALU.subtract,
-                )
+
+        def difference(engine, group, b):
+            engine.tensor_tensor(
+                out=e_tiles[(group, b % 2)][:, b // 2, :],
+                in0=k_copies[(group, b)] if (group, b) in k_copies else big_k[(group, b)][:],
+                in1=max_all[group][:],
+                op=ALU.subtract,
+            )
 
         def pair_in(out, group, parity):
             token_tile, half = divmod(group, HALVES)
@@ -248,22 +243,27 @@ def tile_aftfull_pa_kernel(tc, k, v, Wk, Wv, out_0, out_1):
                 quantise(first_chunks[i - 1])
 
         early, late = chunks_of_period[0]
-        for block in range(BLOCKS):
-            if block == BLOCKS // 2:
-                quantise(first_chunks[-1])
+        for block in range(BLOCKS - 1):
             sort(early, block, nc.vector.tensor_copy)
-        k_products(0, (0, 2, 1, 3))
+        sort(early, BLOCKS - 1, nc.gpsimd.tensor_copy)
+        quantise(first_chunks[-1])
+        k_products(0, (0, 2, 1, 3), (0, 2))
         pair_maxima(0)
-        for block in range(BLOCKS):
+        for block in range(BLOCKS - 1):
             sort(late, block, nc.vector.tensor_copy)
         maximum(0)
-        differences(0)
+        sort(late, BLOCKS - 1, nc.vector.tensor_copy)
+        for b in (1, 3):
+            difference(nc.vector, 0, b)
+        for b in (0, 2):
+            difference(nc.gpsimd, 0, b)
         for block in range(BLOCKS):
             turn(early, block)
-        k_products(1, (0, 2))
-        for block in range(BLOCKS):
+        k_products(1, (0, 2), (0, 2))
+        for block in range(BLOCKS - 1):
             turn(late, block)
-        k_products(1, (1, 3))
+        k_products(1, (1, 3), ())
+        turn(late, BLOCKS - 1)
         exp_and_store(0, 1)
 
         for period in range(1, GROUPS + 1):
@@ -272,37 +272,53 @@ def tile_aftfull_pa_kernel(tc, k, v, Wk, Wv, out_0, out_1):
             has_k = group < GROUPS
             blocks = [(chunk, block) for chunk in chunks_of_period[period] for block in range(BLOCKS)]
             middle = len(blocks) // 2
+            next_chunks = chunks_of_period[period + 1] if has_k else []
             big_v = {}
 
             big_v[1] = product(V_SIDE, v_group, 1)
+            for chunk, block in blocks[:middle]:
+                turn(chunk, block)
+            for chunk in next_chunks:
+                for block in SORTED_BY_SCALAR:
+                    sort(chunk, block, nc.scalar.copy)
+            big_v[3] = product(V_SIDE, v_group, 3)
             if has_k:
                 pair_maxima(group)
             if period == 1:
                 for chunk in chunks_of_period[0]:
                     quantise(chunk)
             multiply(v_group, 1, big_v[1])
-            for chunk, block in blocks[:middle]:
-                turn(chunk, block)
-            big_v[3] = product(V_SIDE, v_group, 3)
             if has_k:
                 maximum(group)
-            multiply(v_group, 3, big_v[3])
-            if period < GROUPS:
-                for chunk in chunks_of_period[period + 1]:
-                    for block in SORTED_BLOCKS:
-                        sort(chunk, block, nc.scalar.copy)
             exp_and_store(v_group, 0)
+            multiply(v_group, 3, big_v[3])
+            on_vector = []
             if has_k:
-                differences(group)
+                for b in (1, 3):
+                    difference(nc.gpsimd if (group, b) in k_copies else nc.vector, group, b)
+                if group == GROUPS - 1:
+                    on_vector = [0]
+                else:
+                    difference(nc.gpsimd, group, 0)
+                    for chunk in next_chunks:
+                        for block in SORTED_BY_GPSIMD.get(period + 1, ()):
+                            sort(chunk, block, nc.gpsimd.tensor_copy)
+                difference(nc.gpsimd, group, 2)
             for chunk, block in blocks[middle:]:
                 turn(chunk, block)
             for b in (0, 2):
                 big_v[b] = product(V_SIDE, v_group, b)
             for b in (0, 2):
                 multiply(v_group, b, big_v[b])
+            for b in on_vector:
+                difference(nc.vector, group, b)
             for chunk in chunks_of_period[period]:
                 quantise(chunk)
-            if group + 1 < GROUPS:
-                k_products(group + 1, (0, 2, 1, 3))
-            if has_k:
+            if group + 1 < GROUPS and not next_chunks:
+                exp_and_store(group, 1)
+                k_products(group + 1, (0, 2, 1, 3), (0, 2, 1))
+            elif group + 1 < GROUPS:
+                k_products(group + 1, (0, 2, 1, 3), (0, 2))
+                exp_and_store(group, 1)
+            elif has_k:
                 exp_and_store(group, 1)

@@ -23,7 +23,7 @@ CHUNK = BLOCKS * P
 N = 512
 HALVES = DH // N
 SORTED_BY_SCALAR = (0,)
-SORTED_BY_GPSIMD = {2: (2, 3)}
+SORTED_BY_GPSIMD = {2: (2, 3), 3: (2, 3)}
 TOKEN_TILES = T // P
 GROUPS = TOKEN_TILES * HALVES
 K_SIDE = 0
@@ -165,10 +165,12 @@ def tile_aftfull_pa_kernel(tc, k, v, Wk, Wv, out_0, out_1):
                 )
             return acc
 
-        def k_products(group, items, copied):
+        def k_products(group, items):
             for b in items:
                 big_k[(group, b)] = product(K_SIDE, group, b)
-            for b in copied:
+
+        def copy_k(group, items):
+            for b in items:
                 if b % 2 == 0:
                     if group not in even_copies:
                         even_copies[group] = work_pool.tile([P, 2, N], F32, name="k_copy")
@@ -247,7 +249,8 @@ def tile_aftfull_pa_kernel(tc, k, v, Wk, Wv, out_0, out_1):
             sort(early, block, nc.vector.tensor_copy)
         sort(early, BLOCKS - 1, nc.gpsimd.tensor_copy)
         quantise(first_chunks[-1])
-        k_products(0, (0, 2, 1, 3), (0, 2))
+        k_products(0, (0, 2, 1, 3))
+        copy_k(0, (0, 2))
         pair_maxima(0)
         for block in range(BLOCKS - 1):
             sort(late, block, nc.vector.tensor_copy)
@@ -259,11 +262,12 @@ def tile_aftfull_pa_kernel(tc, k, v, Wk, Wv, out_0, out_1):
             difference(nc.gpsimd, 0, b)
         for block in range(BLOCKS):
             turn(early, block)
-        k_products(1, (0, 2), (0, 2))
-        for block in range(BLOCKS - 1):
+        k_products(1, (0, 2))
+        copy_k(1, (0, 2))
+        for block in range(BLOCKS):
+            if block == BLOCKS // 2:
+                k_products(1, (1, 3))
             turn(late, block)
-        k_products(1, (1, 3), ())
-        turn(late, BLOCKS - 1)
         exp_and_store(0, 1)
 
         for period in range(1, GROUPS + 1):
@@ -284,6 +288,8 @@ def tile_aftfull_pa_kernel(tc, k, v, Wk, Wv, out_0, out_1):
             big_v[3] = product(V_SIDE, v_group, 3)
             if has_k:
                 pair_maxima(group)
+                if not blocks:
+                    copy_k(group, (1,))
             if period == 1:
                 for chunk in chunks_of_period[0]:
                     quantise(chunk)
@@ -314,11 +320,10 @@ def tile_aftfull_pa_kernel(tc, k, v, Wk, Wv, out_0, out_1):
                 difference(nc.vector, group, b)
             for chunk in chunks_of_period[period]:
                 quantise(chunk)
-            if group + 1 < GROUPS and not next_chunks:
+            if has_k and not next_chunks:
                 exp_and_store(group, 1)
-                k_products(group + 1, (0, 2, 1, 3), (0, 2, 1))
-            elif group + 1 < GROUPS:
-                k_products(group + 1, (0, 2, 1, 3), (0, 2))
-                exp_and_store(group, 1)
-            elif has_k:
+            if group + 1 < GROUPS:
+                k_products(group + 1, (0, 2, 1, 3))
+                copy_k(group + 1, (0, 2))
+            if has_k and next_chunks:
                 exp_and_store(group, 1)

@@ -22,8 +22,7 @@ BLOCKS = 4
 CHUNK = BLOCKS * P
 N = 512
 HALVES = DH // N
-SORTED_BY_SCALAR = (0,)
-SORTED_BY_GPSIMD = {2: (2, 3), 3: (2, 3)}
+SORTED_BLOCKS = (0,)
 TOKEN_TILES = T // P
 GROUPS = TOKEN_TILES * HALVES
 K_SIDE = 0
@@ -245,10 +244,10 @@ def tile_aftfull_pa_kernel(tc, k, v, Wk, Wv, out_0, out_1):
                 quantise(first_chunks[i - 1])
 
         early, late = chunks_of_period[0]
-        for block in range(BLOCKS - 1):
+        for block in range(BLOCKS):
+            if block == BLOCKS - 1:
+                quantise(first_chunks[-1])
             sort(early, block, nc.vector.tensor_copy)
-        sort(early, BLOCKS - 1, nc.gpsimd.tensor_copy)
-        quantise(first_chunks[-1])
         k_products(0, (0, 2, 1, 3))
         copy_k(0, (0, 2))
         pair_maxima(0)
@@ -265,9 +264,8 @@ def tile_aftfull_pa_kernel(tc, k, v, Wk, Wv, out_0, out_1):
         k_products(1, (0, 2))
         copy_k(1, (0, 2))
         for block in range(BLOCKS):
-            if block == BLOCKS // 2:
-                k_products(1, (1, 3))
             turn(late, block)
+        k_products(1, (1, 3))
         exp_and_store(0, 1)
 
         for period in range(1, GROUPS + 1):
@@ -283,13 +281,11 @@ def tile_aftfull_pa_kernel(tc, k, v, Wk, Wv, out_0, out_1):
             for chunk, block in blocks[:middle]:
                 turn(chunk, block)
             for chunk in next_chunks:
-                for block in SORTED_BY_SCALAR:
+                for block in SORTED_BLOCKS:
                     sort(chunk, block, nc.scalar.copy)
             big_v[3] = product(V_SIDE, v_group, 3)
             if has_k:
                 pair_maxima(group)
-                if not blocks:
-                    copy_k(group, (1,))
             if period == 1:
                 for chunk in chunks_of_period[0]:
                     quantise(chunk)
@@ -297,6 +293,8 @@ def tile_aftfull_pa_kernel(tc, k, v, Wk, Wv, out_0, out_1):
             if has_k:
                 maximum(group)
             exp_and_store(v_group, 0)
+            if has_k and not blocks:
+                copy_k(group, (1,))
             multiply(v_group, 3, big_v[3])
             on_vector = []
             if has_k:
@@ -306,9 +304,6 @@ def tile_aftfull_pa_kernel(tc, k, v, Wk, Wv, out_0, out_1):
                     on_vector = [0]
                 else:
                     difference(nc.gpsimd, group, 0)
-                    for chunk in next_chunks:
-                        for block in SORTED_BY_GPSIMD.get(period + 1, ()):
-                            sort(chunk, block, nc.gpsimd.tensor_copy)
                 difference(nc.gpsimd, group, 2)
             for chunk, block in blocks[middle:]:
                 turn(chunk, block)

from contextlib import ExitStack

import concourse.mybir as mybir
from concourse.masks import make_identity

F32 = mybir.dt.float32
BF16 = mybir.dt.bfloat16
U32 = mybir.dt.uint32
U8 = mybir.dt.uint8
FP8X4 = mybir.dt.float8_e4m3fn_x4
ALU = mybir.AluOpType
ACT = mybir.ActivationFunctionType

P = 128
B, T, DM, DH = 4, 512, 1024, 1024
PACK = 4
K_PASS = P * PACK
PASSES = DM // K_PASS
PAIRS = DM // 2
SLOTS = PAIRS // P
BLOCKS = 4
CHUNK = BLOCKS * P
N = 512
HALVES = DH // N
SORTED_BLOCKS = (0,)
TOKEN_TILES = T // P
GROUPS = TOKEN_TILES * HALVES
K_SIDE = 0
V_SIDE = 1

BANKS = {"k0_v1": 1, "k2_v3": 1, "k1": 1, "k3": 1, "turn_v0": 2, "turn_v2": 2}
K_BANK = {0: "k0_v1", 1: "k1", 2: "k2_v3", 3: "k3"}
V_BANK = {0: "turn_v0", 1: "k0_v1", 2: "turn_v2", 3: "k2_v3"}
TURN_BANK = ("turn_v0", "turn_v2")

FLOPS = 2 * 2 * B * T * DM * DH


def chunks_first_used_by(side, group):
    found = []
    if 0 <= group < GROUPS:
        token_tile, half = divmod(group, HALVES)
        if token_tile == 0:
            found.append((side, "weights", half))
        if half == 0:
            found.append((side, "tokens", token_tile))
    return found


def tile_aftfull_pa_kernel(tc, k, v, Wk, Wv, out_0, out_1):
    nc = tc.nc
    tokens = (k, v)
    weights = (Wk, Wv)

    first_chunks = (
        chunks_first_used_by(K_SIDE, 0) + chunks_first_used_by(K_SIDE, 1) + chunks_first_used_by(V_SIDE, 0)
    )
    chunks_of_period = [
        chunks_first_used_by(K_SIDE, period + 2) + chunks_first_used_by(V_SIDE, period + 1)
        for period in range(GROUPS + 1)
    ]
    chunks_of_period[GROUPS - 2] += chunks_of_period[GROUPS - 3]
    chunks_of_period[GROUPS - 3] = []

    with ExitStack() as stack:
        const_pool = stack.enter_context(tc.tile_pool(name="const", bufs=1))
        raw_pool = stack.enter_context(tc.tile_pool(name="raw", bufs=20))
        sorted_pool = stack.enter_context(tc.tile_pool(name="sorted", bufs=4))
        grouped_pool = stack.enter_context(tc.tile_pool(name="grouped", bufs=2))
        mx_pool = stack.enter_context(tc.tile_pool(name="mx", bufs=1))
        work_pool = stack.enter_context(tc.tile_pool(name="work", bufs=2))
        e_pool = stack.enter_context(tc.tile_pool(name="e", bufs=3))
        ev_pool = stack.enter_context(tc.tile_pool(name="ev", bufs=1))
        psum = stack.enter_context(tc.psum_pool(name="psum", bufs=1))

        identity = const_pool.tile([P, P], F32, name="identity")
        make_identity(nc, identity[:])

        stack.enter_context(tc.manual_schedule())

        warm = const_pool.tile([P, 1], F32, name="warm")
        nc.vector.memset(warm[:], 0.0)
        nc.scalar.activation(out=warm[:], in_=warm[:], func=ACT.Exp)

        raw = {}
        sorted_words = {}
        grouped = {}
        codes = {}
        scales = {}
        big_k = {}
        even_copies = {}
        k_copies = {}
        pair_max = {}
        max_all = {}
        e_tiles = {}
        ev_tiles = {}

        def bank(name):
            return psum.tile([P, N], F32, name=name, tag=name, bufs=BANKS[name])

        def load(chunk):
            side, kind, index = chunk
            for block in range(BLOCKS):
                if kind == "weights":
                    first = index * CHUNK + block * P
                    rows = weights[side][first : first + P, :]
                else:
                    rows = tokens[side][block, index * P : (index + 1) * P, :]
                raw[(chunk, block)] = raw_pool.tile([P, DM], BF16, name="raw", tag="raw")
                nc.sync.dma_start(out=raw[(chunk, block)][:], in_=rows)

        def sort(chunk, block, copy):
            sorted_words[(chunk, block)] = sorted_pool.tile([P, PASSES, 2, P], F32, name="sorted", tag="sorted")
            copy(
                out=sorted_words[(chunk, block)][:],
                in_=raw[(chunk, block)][:].bitcast(F32).rearrange("p (g m u) -> p g u m", g=PASSES, u=2),
            )

        def turn(chunk, block):
            if block == 0:
                grouped[chunk] = grouped_pool.tile(
                    [P, PASSES * CHUNK * PACK], BF16, name="grouped", tag="grouped", align_bytes=64
                )
            words = raw[(chunk, block)][:].bitcast(F32)
            turned = bank(TURN_BANK[block % 2])
            for q in range(SLOTS):
                g, u = divmod(q, 2)
                if (chunk, block) in sorted_words:
                    picked = sorted_words[(chunk, block)][:, g, u, :]
                else:
                    picked = words[:, 2 * P * g + u : 2 * P * (g + 1) : 2]
                nc.tensor.transpose(turned[:, q * P : (q + 1) * P], picked, identity[:])
            pairs = grouped[chunk][:].bitcast(F32).rearrange("p (g r u) -> p g r u", g=PASSES, u=2)
            nc.scalar.copy(
                out=pairs[:, :, block * P : (block + 1) * P, :],
                in_=turned[:].rearrange("p (g u r) -> p g r u", g=PASSES, u=2),
            )

        def quantise(chunk):
            name = "%d_%s_%d" % chunk
            codes[chunk] = mx_pool.tile([P, PASSES, CHUNK], U32, name="codes_" + name, align_bytes=64)
            scales[chunk] = mx_pool.tile([P, PASSES, CHUNK], U8, name="scales_" + name, align_bytes=64)
            nc.vector.quantize_mx(
                out=codes[chunk][:].rearrange("p g r -> p (g r)").bitcast(FP8X4),
                scales=scales[chunk][:].rearrange("p g r -> p (g r)"),
                in_=grouped[chunk][:],
            )

        def product(side, group, b):
            token_tile, half = divmod(group, HALVES)
            x = (side, "tokens", token_tile)
            w = (side, "weights", half)
            rows = slice(b * P, (b + 1) * P)
            acc = bank(K_BANK[b] if side == K_SIDE else V_BANK[b])
            for g in range(PASSES):
                nc.tensor.matmul_mx(
                    out=acc[:],
                    lhsT=codes[x][:, g, rows].bitcast(FP8X4),
                    lhsT_scale=scales[x][:, g, rows],
                    rhs=codes[w][:, g, :].bitcast(FP8X4),
                    rhs_scale=scales[w][:, g, :],
                    start=(g == 0),
                    stop=(g == PASSES - 1),
                )
            return acc

        def k_products(group, items):
            for b in items:
                big_k[(group, b)] = product(K_SIDE, group, b)

        def copy_k(group, items):
            for b in items:
                if b % 2 == 0:
                    if group not in even_copies:
                        even_copies[group] = work_pool.tile([P, 2, N], F32, name="k_copy")
                    k_copies[(group, b)] = even_copies[group][:, b // 2, :]
                else:
                    odd_copy = work_pool.tile([P, N], F32, name="k_copy_1", bufs=1)
                    k_copies[(group, b)] = odd_copy[:]
                nc.scalar.copy(out=k_copies[(group, b)], in_=big_k[(group, b)][:])

        def pair_maxima(group):
            pair_max[group] = []
            for first, name in ((0, "max_01"), (2, "max_23")):
                pair = work_pool.tile([P, N], F32, name=name)
                nc.vector.tensor_tensor(
                    out=pair[:], in0=big_k[(group, first + 1)][:], in1=k_copies[(group, first)], op=ALU.max
                )
                pair_max[group].append(pair)

        def maximum(group):
            max_all[group] = work_pool.tile([P, N], F32, name="max_all")
            nc.vector.tensor_tensor(
                out=max_all[group][:], in0=pair_max[group][0][:], in1=pair_max[group][1][:], op=ALU.max
            )
            for parity in (0, 1):
                e_tiles[(group, parity)] = e_pool.tile([P, 2, N], F32, name="e_%d" % parity)

        def difference(engine, group, b):
            engine.tensor_tensor(
                out=e_tiles[(group, b % 2)][:, b // 2, :],
                in0=k_copies[(group, b)] if (group, b) in k_copies else big_k[(group, b)][:],
                in1=max_all[group][:],
                op=ALU.subtract,
            )

        def pair_in(out, group, parity):
            token_tile, half = divmod(group, HALVES)
            part = out[parity:B:2, token_tile * P : (token_tile + 1) * P, half * N : (half + 1) * N]
            return part.rearrange("b p c -> p b c")

        def exp_and_store(group, parity):
            e = e_tiles[(group, parity)]
            flat = e[:].rearrange("p b c -> p (b c)")
            nc.scalar.activation(out=flat, in_=flat, func=ACT.Exp)
            nc.sync.dma_start(out=pair_in(out_1, group, parity), in_=e[:])

        def multiply(group, b, big_v):
            parity = b % 2
            if b == parity:
                ev_tiles[(group, parity)] = ev_pool.tile([P, 2, N], F32, name="ev_%d_%d" % (group, parity))
            nc.vector.tensor_tensor(
                out=ev_tiles[(group, parity)][:, b // 2, :],
                in0=big_v[:],
                in1=e_tiles[(group, parity)][:, b // 2, :],
                op=ALU.mult,
            )
            if group // HALVES == TOKEN_TILES - 1:
                part = pair_in(out_0, group, parity)[:, b // 2, :]
                nc.sync.dma_start(out=part, in_=ev_tiles[(group, parity)][:, b // 2, :])
            elif b == parity + 2:
                nc.sync.dma_start(out=pair_in(out_0, group, parity), in_=ev_tiles[(group, parity)][:])

        for chunk in first_chunks:
            load(chunk)
        for chunks in chunks_of_period:
            for chunk in chunks:
                load(chunk)

        for i, chunk in enumerate(first_chunks):
            for block in range(BLOCKS):
                turn(chunk, block)
            if i > 0:
                quantise(first_chunks[i - 1])

        early, late = chunks_of_period[0]
        for block in range(BLOCKS):
            if block == BLOCKS - 1:
                quantise(first_chunks[-1])
            sort(early, block, nc.vector.tensor_copy)
        k_products(0, (0, 2, 1, 3))
        copy_k(0, (0, 2))
        pair_maxima(0)
        for block in range(BLOCKS - 1):
            sort(late, block, nc.vector.tensor_copy)
        maximum(0)
        sort(late, BLOCKS - 1, nc.vector.tensor_copy)
        for b in (1, 3):
            difference(nc.vector, 0, b)
        for b in (0, 2):
            difference(nc.gpsimd, 0, b)
        for block in range(BLOCKS):
            turn(early, block)
        k_products(1, (0, 2))
        copy_k(1, (0, 2))
        for block in range(BLOCKS):
            turn(late, block)
        k_products(1, (1, 3))
        exp_and_store(0, 1)

        for period in range(1, GROUPS + 1):
            group = period
            v_group = period - 1
            has_k = group < GROUPS
            blocks = [(chunk, block) for chunk in chunks_of_period[period] for block in range(BLOCKS)]
            middle = len(blocks) // 2
            next_chunks = chunks_of_period[period + 1] if has_k else []
            big_v = {}

            big_v[1] = product(V_SIDE, v_group, 1)
            for chunk, block in blocks[:middle]:
                turn(chunk, block)
            for chunk in next_chunks:
                for block in SORTED_BLOCKS:
                    sort(chunk, block, nc.scalar.copy)
            big_v[3] = product(V_SIDE, v_group, 3)
            if has_k:
                pair_maxima(group)
            if period == 1:
                for chunk in chunks_of_period[0]:
                    quantise(chunk)
            multiply(v_group, 1, big_v[1])
            if has_k:
                maximum(group)
            exp_and_store(v_group, 0)
            if has_k and not blocks:
                copy_k(group, (1,))
            multiply(v_group, 3, big_v[3])
            on_vector = []
            if has_k:
                for b in (1, 3):
                    difference(nc.gpsimd if (group, b) in k_copies else nc.vector, group, b)
                if group == GROUPS - 1:
                    on_vector = [0]
                else:
                    difference(nc.gpsimd, group, 0)
                difference(nc.gpsimd, group, 2)
            for chunk, block in blocks[middle:]:
                turn(chunk, block)
            for b in (0, 2):
                big_v[b] = product(V_SIDE, v_group, b)
            for b in (0, 2):
                multiply(v_group, b, big_v[b])
            for b in on_vector:
                difference(nc.vector, group, b)
            for chunk in chunks_of_period[period]:
                quantise(chunk)
            if has_k and not next_chunks:
                exp_and_store(group, 1)
            if group + 1 < GROUPS:
                k_products(group + 1, (0, 2, 1, 3))
                copy_k(group + 1, (0, 2))
            if has_k and next_chunks:
                exp_and_store(group, 1)
